import numpy as np
import ml_dtypes


def mxq(x, axis, fmt="e4m3"):
    dtype, down = {"e4m3": (ml_dtypes.float8_e4m3fn, 7), "e5m2": (ml_dtypes.float8_e5m2, 14)}[fmt]
    v = np.moveaxis(np.asarray(x, np.float32).astype(ml_dtypes.bfloat16).astype(np.float64), axis, -1)
    blocks = v.reshape(v.shape[:-1] + (-1, 32))
    amax = np.abs(blocks).max(-1, keepdims=True)
    byte = np.maximum(np.where(amax > 0, np.frexp(amax)[1] - 1 + 127, 0) - down, 1)
    scale = np.exp2(byte - 127.0)
    codes = (blocks / scale).astype(np.float32).astype(dtype).astype(np.float64)
    return np.moveaxis((codes * scale).reshape(v.shape), -1, axis)


WIDE = False


def mx_kscale(k):
    if not WIDE:
        return np.ones(k)
    levels = np.array([10, -10, 5, -5, 0])
    if k % 512:
        return np.exp2(np.random.permutation(np.resize(levels, k // 32))).repeat(32)
    a = np.empty((k // 512, 16))
    for p in range(k // 512):
        a[p, :8] = np.random.permutation(np.resize(levels, 8))
        for g in range(8):
            far = levels[np.abs(levels - a[p, g]) >= 10]
            a[p, g + 8] = far[np.random.randint(len(far))]
    return np.exp2(a.ravel()).repeat(32)


BF16 = ml_dtypes.bfloat16


def bf(x):
    return np.asarray(x, np.float32).astype(BF16)


def f64(x):
    return np.asarray(x).astype(np.float64)


B, N, E, H, G, C, EO = 4, 2048, 512, 8, 128, 512, 128
LN_EPS = 1e-5


def sigmoid(v):
    return 1.0 / (1.0 + np.exp(-v))


def layernorm(y, w, b):
    mu = y.mean(-1, keepdims=True)
    var = np.square(y - mu).mean(-1, keepdims=True)
    return (y - mu) / np.sqrt(var + LN_EPS) * w + b


def setup_inputs():
    s = mx_kscale(E)
    return {"attn": bf((1.5 + 2.5 * np.random.standard_normal((B, N, E))) * s),
            "gate_low": bf(np.random.standard_normal((B, N, G))),
            "Wg2": bf(np.random.standard_normal((G, E)) / np.sqrt(G)),
            "Wo": bf(np.random.standard_normal((E, EO)) / np.sqrt(E) / s[:, None]),
            "ln_w": bf(1.0 + 0.1 * np.random.standard_normal(EO)),
            "ln_b": bf(0.1 * np.random.standard_normal(EO))}


def reference(attn, gate_low, Wg2, Wo, ln_w, ln_b):
    gate = sigmoid(f64(gate_low) @ f64(Wg2))
    h = f64(attn) * gate
    y = mxq(h, 2, "e4m3") @ mxq(f64(Wo), 0, "e4m3")
    return layernorm(y, f64(ln_w), f64(ln_b))

@@ -1,0 +1,329 @@
+from contextlib import ExitStack
+
+import concourse.mybir as mybir
+from concourse.masks import make_identity
+
+F32 = mybir.dt.float32
+BF16 = mybir.dt.bfloat16
+U32 = mybir.dt.uint32
+U8 = mybir.dt.uint8
+FP8X4 = mybir.dt.float8_e4m3fn_x4
+ACT = mybir.ActivationFunctionType
+ALU = mybir.AluOpType
+
+P = 128
+PACK = 4
+TOKENS = 4 * 2048
+E = 512
+G = 128
+EO = 128
+LN_EPS = 1e-5
+
+PAIR_TILES = 2
+QUAD_TILES = 4
+CHUNK_TILES = 8
+PAIR = PAIR_TILES * P
+QUAD = QUAD_TILES * P
+CHUNK = CHUNK_TILES * P
+N_CHUNKS = TOKENS // CHUNK
+N_QUADS = TOKENS // QUAD
+N_PAIRS = TOKENS // PAIR
+PAIRS_PER_CHUNK = CHUNK_TILES // PAIR_TILES
+PAIRS_PER_QUAD = QUAD_TILES // PAIR_TILES
+QUADS_PER_CHUNK = CHUNK_TILES // QUAD_TILES
+BN_STATS = 6
+BN_AGGR = 2
+
+GATE_LOW_LEAD = 2
+MULTIPLY_LAG = 1
+QUANTISE_LAG = 3
+PROJECT_LAG = 4
+STATS_LAG = 5
+RSTD_LAG = 6
+NORMALISE_LAG = 8
+SCALE_LAG = 10
+
+FLOPS = 2 * TOKENS * G * E + 2 * TOKENS * E * EO
+
+
+def tile_tnlattention_pb_t_kernel(tc, attn, gate_low, Wg2, Wo, ln_w, ln_b, out):
+    nc = tc.nc
+    attn_rows = attn.flatten_outer_dims()
+    gate_low_rows = gate_low.flatten_outer_dims()
+    out_rows = out.flatten_outer_dims()
+
+    def chunk_view(rows, c):
+        return rows[c * CHUNK : (c + 1) * CHUNK, :].rearrange("(p j) w -> p j w", j=CHUNK_TILES)
+
+    with ExitStack() as ctx:
+        consts = ctx.enter_context(tc.tile_pool(name="consts", bufs=1))
+        attn_pool = ctx.enter_context(tc.tile_pool(name="attn", bufs=N_QUADS))
+        gate_low_pool = ctx.enter_context(tc.tile_pool(name="gate_low", bufs=N_CHUNKS))
+        gate_low_t_pool = ctx.enter_context(tc.tile_pool(name="gate_low_t", bufs=2))
+        gate_pool = ctx.enter_context(tc.tile_pool(name="gate", bufs=3))
+        h_pool = ctx.enter_context(tc.tile_pool(name="h", bufs=3))
+        mx_pool = ctx.enter_context(tc.tile_pool(name="mx", bufs=3))
+        stat_pool = ctx.enter_context(tc.tile_pool(name="stat", bufs=4))
+        result_pool = ctx.enter_context(tc.tile_pool(name="result", bufs=6))
+        for_scalar_psum = ctx.enter_context(tc.psum_pool(name="for_scalar_ps", bufs=3))
+        attn_t_psum = ctx.enter_context(tc.psum_pool(name="attn_t_ps", bufs=2))
+        y_psum = ctx.enter_context(tc.psum_pool(name="y_ps", bufs=3))
+
+        wg2_sb = consts.tile([P, E], BF16)
+        nc.sync.dma_start(out=wg2_sb[:], in_=Wg2[:, :])
+        wo_rows = consts.tile([P, PACK, EO], BF16)
+        ln_w_bf16 = consts.tile([P, EO], BF16)
+        ln_b_bf16 = consts.tile([P, EO], BF16)
+        attn_quads = []
+        gate_low_chunks = []
+        for c in range(N_CHUNKS):
+            gate_low_sb = gate_low_pool.tile([P, CHUNK_TILES, G], BF16)
+            nc.sync.dma_start(out=gate_low_sb[:], in_=chunk_view(gate_low_rows, c))
+            gate_low_chunks.append(gate_low_sb)
+            for half in range(QUADS_PER_CHUNK):
+                tiles = slice(half * QUAD_TILES, (half + 1) * QUAD_TILES)
+                attn_sb = attn_pool.tile([P, QUAD_TILES, E], BF16)
+                nc.sync.dma_start(out=attn_sb[:], in_=chunk_view(attn_rows, c)[:, tiles, :])
+                attn_quads.append(attn_sb)
+            if c == 0:
+                nc.sync.dma_start(
+                    out=wo_rows[:], in_=Wo.rearrange("(q t) o -> q t o", t=PACK)
+                )
+                nc.sync.dma_start(out=ln_w_bf16[:], in_=ln_w.partition_broadcast(P))
+                nc.sync.dma_start(out=ln_b_bf16[:], in_=ln_b.partition_broadcast(P))
+
+        ident_bf16 = consts.tile([P, P], BF16)
+        make_identity(nc, ident_bf16[:])
+        ident_f32 = consts.tile([P, P], F32)
+        make_identity(nc, ident_f32[:])
+        minus_half = consts.tile([P, QUAD_TILES], F32)
+        nc.vector.memset(minus_half[:], -0.5)
+        warm = consts.tile([P, 1], F32)
+        nc.vector.memset(warm[:], 0.0)
+        nc.scalar.activation(out=warm[:], in_=warm[:], func=ACT.Sigmoid)
+
+        wg2_by_t = consts.tile([P, PACK, P], BF16)
+        nc.vector.tensor_copy(
+            out=wg2_by_t[:], in_=wg2_sb[:].rearrange("g (q t) -> g t q", t=PACK)
+        )
+
+        wo_codes = consts.tile([P, EO], U32, align_bytes=64)
+        wo_scales = consts.tile([P, EO], U8, align_bytes=64)
+        ln_w_quad = consts.tile([P, QUAD_TILES, EO], F32)
+        ln_b_quad = consts.tile([P, QUAD_TILES, EO], F32)
+
+        def spread_ln_w_and_b():
+            whole = [P, QUAD_TILES, EO]
+            nc.vector.tensor_copy(out=ln_w_quad[:], in_=ln_w_bf16[:].unsqueeze(1).to_broadcast(whole))
+            nc.vector.tensor_copy(out=ln_b_quad[:], in_=ln_b_bf16[:].unsqueeze(1).to_broadcast(whole))
+
+        def quantise_wo():
+            wo_grouped = consts.tile([P, EO, PACK], BF16, align_bytes=64)
+            nc.vector.tensor_copy(out=wo_grouped[:], in_=wo_rows[:].rearrange("q t o -> q o t"))
+            nc.vector.quantize_mx(
+                out=wo_codes[:].bitcast(FP8X4),
+                scales=wo_scales[:],
+                in_=wo_grouped[:].rearrange("q o t -> q (o t)"),
+            )
+
+        gate_low_t = {}
+        gate = {}
+        attn_t = {}
+        h = {}
+        h_codes = {}
+        h_scales = {}
+        y = {}
+        mean_var = {}
+        rstd = {}
+        shift = {}
+
+        normalised = {}
+
+        def by_vector(quad):
+            return quad == N_QUADS - 1
+
+        def transpose_gate_low(c):
+            gate_low_t_ps = for_scalar_psum.tile([P, CHUNK], BF16, tag="for_scalar")
+            for j in range(CHUNK_TILES):
+                nc.tensor.transpose(
+                    gate_low_t_ps[:, j * P : (j + 1) * P], gate_low_chunks[c][:, j, :], ident_bf16[:]
+                )
+            gate_low_t_sb = gate_low_t_pool.tile([P, CHUNK], BF16)
+            nc.scalar.copy(out=gate_low_t_sb[:], in_=gate_low_t_ps[:])
+            gate_low_t[c] = gate_low_t_sb
+
+        def compute_gate(s):
+            c = s // PAIRS_PER_CHUNK
+            first_tile = (s % PAIRS_PER_CHUNK) * PAIR_TILES
+            gate_sb = gate_pool.tile([P, PAIR, PACK], F32)
+            for i in range(PAIR_TILES):
+                tokens = slice((first_tile + i) * P, (first_tile + i + 1) * P)
+                z_ps = for_scalar_psum.tile([P, PACK, P], F32, tag="for_scalar")
+                for t in range(PACK):
+                    nc.tensor.matmul(
+                        out=z_ps[:, t, :], lhsT=wg2_by_t[:, t, :], rhs=gate_low_t[c][:, tokens],
+                        start=True, stop=True,
+                    )
+                nc.scalar.activation(
+                    out=gate_sb[:, i * P : (i + 1) * P, :],
+                    in_=z_ps[:].rearrange("q t n -> q n t"),
+                    func=ACT.Sigmoid,
+                )
+            gate[s] = gate_sb
+
+        def transpose_attn(s):
+            first_tile = (s % PAIRS_PER_QUAD) * PAIR_TILES
+            attn_t_ps = attn_t_psum.tile([P, 2, PAIR], F32)
+            for i in range(PAIR_TILES):
+                words = attn_quads[s // PAIRS_PER_QUAD][:, first_tile + i, :].bitcast(F32)
+                for u in range(2):
+                    nc.tensor.transpose(
+                        attn_t_ps[:, u, i * P : (i + 1) * P], words[:, u : 2 * P : 2], ident_f32[:]
+                    )
+            attn_t[s] = attn_t_ps
+
+        def multiply(s):
+            quad = s // PAIRS_PER_QUAD
+            if s % PAIRS_PER_QUAD == 0:
+                h_sb = h_pool.tile([P, QUAD, PACK], BF16, align_bytes=64)
+                h[quad] = h_sb
+            tokens = slice((s % PAIRS_PER_QUAD) * PAIR, (s % PAIRS_PER_QUAD + 1) * PAIR)
+            nc.vector.tensor_tensor(
+                out=h[quad][:, tokens, :].rearrange("q n (u e) -> q n u e", e=2),
+                in0=attn_t[s][:].bitcast(BF16).rearrange("q u (n e) -> q n u e", e=2),
+                in1=gate[s][:].rearrange("q n (u e) -> q n u e", e=2),
+                op=ALU.mult,
+            )
+
+        def quantise(quad):
+            codes = mx_pool.tile([P, QUAD], U32, align_bytes=64)
+            scales = mx_pool.tile([P, QUAD], U8, align_bytes=64)
+            nc.vector.quantize_mx(
+                out=codes[:].bitcast(FP8X4),
+                scales=scales[:],
+                in_=h[quad][:].rearrange("q n t -> q (n t)"),
+            )
+            h_codes[quad] = codes
+            h_scales[quad] = scales
+
+        def project(quad):
+            y_ps = y_psum.tile([P, QUAD_TILES, EO], F32)
+            for i in range(QUAD_TILES):
+                tokens = slice(i * P, (i + 1) * P)
+                nc.tensor.matmul_mx(
+                    out=y_ps[:, i, :],
+                    lhsT=h_codes[quad][:, tokens].bitcast(FP8X4),
+                    lhsT_scale=h_scales[quad][:, tokens],
+                    rhs=wo_codes[:].bitcast(FP8X4),
+                    rhs_scale=wo_scales[:],
+                    start=True,
+                    stop=True,
+                )
+            y[quad] = y_ps
+
+        def statistics(quad):
+            stats = stat_pool.tile([P, QUAD_TILES, BN_STATS], F32)
+            mean_var_sb = stat_pool.tile([P, QUAD_TILES, BN_AGGR], F32)
+            for i in range(QUAD_TILES):
+                nc.vector.bn_stats(out=stats[:, i, :], in_=y[quad][:, i, :])
+            for i in range(QUAD_TILES):
+                nc.vector.bn_aggr(out=mean_var_sb[:, i, :], in_=stats[:, i, :])
+            mean_var[quad] = mean_var_sb
+
+        def compute_rstd(quad):
+            var_eps = stat_pool.tile([P, QUAD_TILES], F32)
+            nc.scalar.activation(
+                out=var_eps[:], in_=mean_var[quad][:, :, 1], func=ACT.Identity, bias=LN_EPS, scale=1.0
+            )
+            rstd_sb = stat_pool.tile([P, QUAD_TILES], F32)
+            nc.gpsimd.tensor_tensor(out=rstd_sb[:], in0=var_eps[:], in1=minus_half[:], op=ALU.pow)
+            rstd[quad] = rstd_sb
+            if not by_vector(quad):
+                neg_mean = stat_pool.tile([P, QUAD_TILES], F32)
+                nc.scalar.mul(out=neg_mean[:], in_=mean_var[quad][:, :, 0], mul=-1.0)
+                shift_sb = stat_pool.tile([P, QUAD_TILES], F32)
+                nc.gpsimd.tensor_tensor(out=shift_sb[:], in0=neg_mean[:], in1=rstd_sb[:], op=ALU.mult)
+                shift[quad] = shift_sb
+
+        def store(quad, result):
+            first_tile = (quad % QUADS_PER_CHUNK) * QUAD_TILES
+            nc.sync.dma_start(
+                out=chunk_view(out_rows, quad // QUADS_PER_CHUNK)[:, first_tile : first_tile + QUAD_TILES, :],
+                in_=result[:],
+            )
+
+        def normalise(quad):
+            normalised_sb = result_pool.tile([P, QUAD_TILES, EO], F32)
+            for i in range(QUAD_TILES):
+                nc.scalar.activation(
+                    out=normalised_sb[:, i, :], in_=y[quad][:, i, :], func=ACT.Identity,
+                    bias=shift[quad][:, i : i + 1], scale=rstd[quad][:, i : i + 1],
+                )
+            normalised[quad] = normalised_sb
+
+        def scale_and_store(quad):
+            result = result_pool.tile([P, QUAD_TILES, EO], F32)
+            nc.vector.tensor_tensor(out=result[:], in0=normalised[quad][:], in1=ln_w_quad[:], op=ALU.mult)
+            nc.gpsimd.tensor_tensor(out=result[:], in0=result[:], in1=ln_b_quad[:], op=ALU.add)
+            store(quad, result)
+
+        def finish_on_vector(quad):
+            centred = result_pool.tile([P, QUAD_TILES, EO], F32)
+            result = result_pool.tile([P, QUAD_TILES, EO], F32)
+            for i in range(QUAD_TILES):
+                nc.vector.scalar_tensor_tensor(
+                    out=centred[:, i, :], in0=y[quad][:, i, :], scalar=mean_var[quad][:, i, 0:1],
+                    in1=ln_w_quad[:, i, :], op0=ALU.subtract, op1=ALU.mult,
+                )
+            for i in range(QUAD_TILES):
+                nc.vector.scalar_tensor_tensor(
+                    out=result[:, i, :], in0=centred[:, i, :], scalar=rstd[quad][:, i : i + 1],
+                    in1=ln_b_quad[:, i, :], op0=ALU.mult, op1=ALU.add,
+                )
+            store(quad, result)
+
+        def pair_due(step, lag):
+            s = step - lag
+            return s if 0 <= s < N_PAIRS else None
+
+        def quad_due(step, lag):
+            quad, rest = divmod(step - lag, PAIRS_PER_QUAD)
+            return quad if rest == 0 and 0 <= quad < N_QUADS else None
+
+        with tc.manual_schedule():
+            transpose_gate_low(0)
+            for step in range(N_PAIRS + SCALE_LAG):
+                s = pair_due(step, 0)
+                if s is not None:
+                    compute_gate(s)
+                    transpose_attn(s)
+                ahead = pair_due(step, -GATE_LOW_LEAD)
+                if ahead is not None and ahead % PAIRS_PER_CHUNK == 0:
+                    transpose_gate_low(ahead // PAIRS_PER_CHUNK)
+                quad = quad_due(step, PROJECT_LAG)
+                if quad is not None:
+                    project(quad)
+                quad = quad_due(step, RSTD_LAG)
+                if quad is not None:
+                    compute_rstd(quad)
+                s = pair_due(step, MULTIPLY_LAG)
+                if s is not None:
+                    multiply(s)
+                if step == QUANTISE_LAG:
+                    quantise_wo()
+                    spread_ln_w_and_b()
+                quad = quad_due(step, QUANTISE_LAG)
+                if quad is not None:
+                    quantise(quad)
+                quad = quad_due(step, STATS_LAG)
+                if quad is not None:
+                    statistics(quad)
+                quad = quad_due(step, SCALE_LAG)
+                if quad is not None and not by_vector(quad):
+                    scale_and_store(quad)
+                quad = quad_due(step, NORMALISE_LAG)
+                if quad is not None:
+                    if by_vector(quad):
+                        finish_on_vector(quad)
+                    else:
+                        normalise(quad)

@@ -31,8 +31,9 @@ N_PAIRS = TOKENS // PAIR
 PAIRS_PER_CHUNK = CHUNK_TILES // PAIR_TILES
 PAIRS_PER_QUAD = QUAD_TILES // PAIR_TILES
 QUADS_PER_CHUNK = CHUNK_TILES // QUAD_TILES
-BN_STATS = 6
-BN_AGGR = 2
+BN_VALUES = 3
+BN_MEAN = 1
+BN_SUM_OF_SQUARES = 2
 
 GATE_LOW_LEAD = 2
 MULTIPLY_LAG = 1
@@ -133,7 +134,7 @@ def tile_tnlattention_pb_t_kernel(tc, attn, gate_low, Wg2, Wo, ln_w, ln_b, out):
         h_codes = {}
         h_scales = {}
         y = {}
-        mean_var = {}
+        stats = {}
         rstd = {}
         shift = {}
 
@@ -222,25 +223,26 @@ def tile_tnlattention_pb_t_kernel(tc, attn, gate_low, Wg2, Wo, ln_w, ln_b, out):
             y[quad] = y_ps
 
         def statistics(quad):
-            stats = stat_pool.tile([P, QUAD_TILES, BN_STATS], F32)
-            mean_var_sb = stat_pool.tile([P, QUAD_TILES, BN_AGGR], F32)
-            for i in range(QUAD_TILES):
-                nc.vector.bn_stats(out=stats[:, i, :], in_=y[quad][:, i, :])
-            for i in range(QUAD_TILES):
-                nc.vector.bn_aggr(out=mean_var_sb[:, i, :], in_=stats[:, i, :])
-            mean_var[quad] = mean_var_sb
+            stats_sb = stat_pool.tile([P, QUAD_TILES, BN_VALUES], F32)
+            for i in range(0, QUAD_TILES, 2):
+                nc.vector.bn_stats(
+                    out=stats_sb[:, i : i + 2, :].rearrange("p x v -> p (x v)"),
+                    in_=y[quad][:, i : i + 2, :].rearrange("p x o -> p o x"),
+                )
+            stats[quad] = stats_sb
 
         def compute_rstd(quad):
             var_eps = stat_pool.tile([P, QUAD_TILES], F32)
             nc.scalar.activation(
-                out=var_eps[:], in_=mean_var[quad][:, :, 1], func=ACT.Identity, bias=LN_EPS, scale=1.0
+                out=var_eps[:], in_=stats[quad][:, :, BN_SUM_OF_SQUARES], func=ACT.Identity,
+                bias=LN_EPS, scale=1.0 / EO,
             )
             rstd_sb = stat_pool.tile([P, QUAD_TILES], F32)
             nc.gpsimd.tensor_tensor(out=rstd_sb[:], in0=var_eps[:], in1=minus_half[:], op=ALU.pow)
             rstd[quad] = rstd_sb
             if not by_vector(quad):
                 neg_mean = stat_pool.tile([P, QUAD_TILES], F32)
-                nc.scalar.mul(out=neg_mean[:], in_=mean_var[quad][:, :, 0], mul=-1.0)
+                nc.scalar.mul(out=neg_mean[:], in_=stats[quad][:, :, BN_MEAN], mul=-1.0)
                 shift_sb = stat_pool.tile([P, QUAD_TILES], F32)
                 nc.gpsimd.tensor_tensor(out=shift_sb[:], in0=neg_mean[:], in1=rstd_sb[:], op=ALU.mult)
                 shift[quad] = shift_sb
@@ -272,7 +274,7 @@ def tile_tnlattention_pb_t_kernel(tc, attn, gate_low, Wg2, Wo, ln_w, ln_b, out):
             result = result_pool.tile([P, QUAD_TILES, EO], F32)
             for i in range(QUAD_TILES):
                 nc.vector.scalar_tensor_tensor(
-                    out=centred[:, i, :], in0=y[quad][:, i, :], scalar=mean_var[quad][:, i, 0:1],
+                    out=centred[:, i, :], in0=y[quad][:, i, :], scalar=stats[quad][:, i, BN_MEAN : BN_MEAN + 1],
                     in1=ln_w_quad[:, i, :], op0=ALU.subtract, op1=ALU.mult,
                 )
             for i in range(QUAD_TILES):

@@ -41,8 +41,8 @@ QUANTISE_LAG = 3
 PROJECT_LAG = 4
 STATS_LAG = 5
 RSTD_LAG = 6
-NORMALISE_LAG = 8
-SCALE_LAG = 10
+CENTRE_LAG = 6
+FINISH_LAG = 8
 
 FLOPS = 2 * TOKENS * G * E + 2 * TOKENS * E * EO
 
@@ -136,12 +136,7 @@ def tile_tnlattention_pb_t_kernel(tc, attn, gate_low, Wg2, Wo, ln_w, ln_b, out):
         y = {}
         stats = {}
         rstd = {}
-        shift = {}
-
-        normalised = {}
-
-        def by_vector(quad):
-            return quad == N_QUADS - 1
+        centred = {}
 
         def transpose_gate_low(c):
             gate_low_t_ps = for_scalar_psum.tile([P, CHUNK], BF16, tag="for_scalar")
@@ -240,12 +235,6 @@ def tile_tnlattention_pb_t_kernel(tc, attn, gate_low, Wg2, Wo, ln_w, ln_b, out):
             rstd_sb = stat_pool.tile([P, QUAD_TILES], F32)
             nc.gpsimd.tensor_tensor(out=rstd_sb[:], in0=var_eps[:], in1=minus_half[:], op=ALU.pow)
             rstd[quad] = rstd_sb
-            if not by_vector(quad):
-                neg_mean = stat_pool.tile([P, QUAD_TILES], F32)
-                nc.scalar.mul(out=neg_mean[:], in_=stats[quad][:, :, BN_MEAN], mul=-1.0)
-                shift_sb = stat_pool.tile([P, QUAD_TILES], F32)
-                nc.gpsimd.tensor_tensor(out=shift_sb[:], in0=neg_mean[:], in1=rstd_sb[:], op=ALU.mult)
-                shift[quad] = shift_sb
 
         def store(quad, result):
             first_tile = (quad % QUADS_PER_CHUNK) * QUAD_TILES
@@ -254,32 +243,31 @@ def tile_tnlattention_pb_t_kernel(tc, attn, gate_low, Wg2, Wo, ln_w, ln_b, out):
                 in_=result[:],
             )
 
-        def normalise(quad):
-            normalised_sb = result_pool.tile([P, QUAD_TILES, EO], F32)
+        def centre(quad):
+            centred_sb = result_pool.tile([P, QUAD_TILES, EO], F32)
+            for i in range(QUAD_TILES):
+                nc.vector.scalar_tensor_tensor(
+                    out=centred_sb[:, i, :], in0=y[quad][:, i, :],
+                    scalar=stats[quad][:, i, BN_MEAN : BN_MEAN + 1],
+                    in1=ln_w_quad[:, i, :], op0=ALU.subtract, op1=ALU.mult,
+                )
+            centred[quad] = centred_sb
+
+        def finish(quad):
+            result = result_pool.tile([P, QUAD_TILES, EO], F32)
             for i in range(QUAD_TILES):
                 nc.scalar.activation(
-                    out=normalised_sb[:, i, :], in_=y[quad][:, i, :], func=ACT.Identity,
-                    bias=shift[quad][:, i : i + 1], scale=rstd[quad][:, i : i + 1],
+                    out=result[:, i, :], in_=centred[quad][:, i, :], func=ACT.Copy,
+                    scale=rstd[quad][:, i : i + 1],
                 )
-            normalised[quad] = normalised_sb
-
-        def scale_and_store(quad):
-            result = result_pool.tile([P, QUAD_TILES, EO], F32)
-            nc.vector.tensor_tensor(out=result[:], in0=normalised[quad][:], in1=ln_w_quad[:], op=ALU.mult)
             nc.gpsimd.tensor_tensor(out=result[:], in0=result[:], in1=ln_b_quad[:], op=ALU.add)
             store(quad, result)
 
         def finish_on_vector(quad):
-            centred = result_pool.tile([P, QUAD_TILES, EO], F32)
             result = result_pool.tile([P, QUAD_TILES, EO], F32)
             for i in range(QUAD_TILES):
                 nc.vector.scalar_tensor_tensor(
-                    out=centred[:, i, :], in0=y[quad][:, i, :], scalar=stats[quad][:, i, BN_MEAN : BN_MEAN + 1],
-                    in1=ln_w_quad[:, i, :], op0=ALU.subtract, op1=ALU.mult,
-                )
-            for i in range(QUAD_TILES):
-                nc.vector.scalar_tensor_tensor(
-                    out=result[:, i, :], in0=centred[:, i, :], scalar=rstd[quad][:, i : i + 1],
+                    out=result[:, i, :], in0=centred[quad][:, i, :], scalar=rstd[quad][:, i : i + 1],
                     in1=ln_b_quad[:, i, :], op0=ALU.mult, op1=ALU.add,
                 )
             store(quad, result)
@@ -294,7 +282,7 @@ def tile_tnlattention_pb_t_kernel(tc, attn, gate_low, Wg2, Wo, ln_w, ln_b, out):
 
         with tc.manual_schedule():
             transpose_gate_low(0)
-            for step in range(N_PAIRS + SCALE_LAG):
+            for step in range(N_PAIRS + FINISH_LAG):
                 s = pair_due(step, 0)
                 if s is not None:
                     compute_gate(s)
@@ -320,12 +308,12 @@ def tile_tnlattention_pb_t_kernel(tc, attn, gate_low, Wg2, Wo, ln_w, ln_b, out):
                 quad = quad_due(step, STATS_LAG)
                 if quad is not None:
                     statistics(quad)
-                quad = quad_due(step, SCALE_LAG)
-                if quad is not None and not by_vector(quad):
-                    scale_and_store(quad)
-                quad = quad_due(step, NORMALISE_LAG)
+                quad = quad_due(step, CENTRE_LAG)
                 if quad is not None:
-                    if by_vector(quad):
+                    centre(quad)
+                quad = quad_due(step, FINISH_LAG)
+                if quad is not None:
+                    if quad == N_QUADS - 1:
                         finish_on_vector(quad)
                     else:
-                        normalise(quad)
+                        finish(quad)

@@ -35,14 +35,20 @@ BN_VALUES = 3
 BN_MEAN = 1
 BN_SUM_OF_SQUARES = 2
 
+FIRST_TILES = slice(0, PAIR_TILES)
 GATE_LOW_LEAD = 2
 MULTIPLY_LAG = 1
-QUANTISE_LAG = 3
-PROJECT_LAG = 4
-STATS_LAG = 5
-RSTD_LAG = 6
-CENTRE_LAG = 6
-FINISH_LAG = 8
+QUANTISE_LAG = 2
+PROJECT_LAG = 3
+STATS_LAG = 4
+RSTD_LAG = 5
+CENTRE_LAG = 5
+FINISH_LAG = 7
+
+GROUPS = [(s, PAIRS_PER_QUAD) for s in range(0, N_PAIRS - PAIRS_PER_QUAD, PAIRS_PER_QUAD)] + [
+    (s, 1) for s in range(N_PAIRS - PAIRS_PER_QUAD, N_PAIRS)
+]
+FIRST_GROUP_BY_VECTOR = len(GROUPS) - 3
 
 FLOPS = 2 * TOKENS * G * E + 2 * TOKENS * E * EO
 
@@ -71,7 +77,6 @@ def tile_tnlattention_pb_t_kernel(tc, attn, gate_low, Wg2, Wo, ln_w, ln_b, out):
         y_psum = ctx.enter_context(tc.psum_pool(name="y_ps", bufs=3))
 
         wg2_sb = consts.tile([P, E], BF16)
-        nc.sync.dma_start(out=wg2_sb[:], in_=Wg2[:, :])
         wo_rows = consts.tile([P, PACK, EO], BF16)
         ln_w_bf16 = consts.tile([P, EO], BF16)
         ln_b_bf16 = consts.tile([P, EO], BF16)
@@ -79,19 +84,36 @@ def tile_tnlattention_pb_t_kernel(tc, attn, gate_low, Wg2, Wo, ln_w, ln_b, out):
         gate_low_chunks = []
         for c in range(N_CHUNKS):
             gate_low_sb = gate_low_pool.tile([P, CHUNK_TILES, G], BF16)
-            nc.sync.dma_start(out=gate_low_sb[:], in_=chunk_view(gate_low_rows, c))
             gate_low_chunks.append(gate_low_sb)
             for half in range(QUADS_PER_CHUNK):
-                tiles = slice(half * QUAD_TILES, (half + 1) * QUAD_TILES)
                 attn_sb = attn_pool.tile([P, QUAD_TILES, E], BF16)
-                nc.sync.dma_start(out=attn_sb[:], in_=chunk_view(attn_rows, c)[:, tiles, :])
                 attn_quads.append(attn_sb)
-            if c == 0:
-                nc.sync.dma_start(
-                    out=wo_rows[:], in_=Wo.rearrange("(q t) o -> q t o", t=PACK)
-                )
-                nc.sync.dma_start(out=ln_w_bf16[:], in_=ln_w.partition_broadcast(P))
-                nc.sync.dma_start(out=ln_b_bf16[:], in_=ln_b.partition_broadcast(P))
+
+        def load_gate_low(c, tiles):
+            nc.sync.dma_start(out=gate_low_chunks[c][:, tiles, :], in_=chunk_view(gate_low_rows, c)[:, tiles, :])
+
+        def load_attn(quad, tiles):
+            first_tile = (quad % QUADS_PER_CHUNK) * QUAD_TILES
+            nc.sync.dma_start(
+                out=attn_quads[quad][:, tiles, :],
+                in_=chunk_view(attn_rows, quad // QUADS_PER_CHUNK)[
+                    :, first_tile + tiles.start : first_tile + tiles.stop, :
+                ],
+            )
+
+        load_gate_low(0, FIRST_TILES)
+        nc.sync.dma_start(out=wg2_sb[:], in_=Wg2[:, :])
+        load_attn(0, FIRST_TILES)
+        load_gate_low(0, slice(PAIR_TILES, CHUNK_TILES))
+        load_attn(0, slice(PAIR_TILES, QUAD_TILES))
+        nc.sync.dma_start(out=wo_rows[:], in_=Wo.rearrange("(q t) o -> q t o", t=PACK))
+        load_attn(1, slice(0, QUAD_TILES))
+        nc.sync.dma_start(out=ln_w_bf16[:], in_=ln_w.partition_broadcast(P))
+        nc.sync.dma_start(out=ln_b_bf16[:], in_=ln_b.partition_broadcast(P))
+        for c in range(1, N_CHUNKS):
+            load_gate_low(c, slice(0, CHUNK_TILES))
+            for half in range(QUADS_PER_CHUNK):
+                load_attn(c * QUADS_PER_CHUNK + half, slice(0, QUAD_TILES))
 
         ident_bf16 = consts.tile([P, P], BF16)
         make_identity(nc, ident_bf16[:])
@@ -113,19 +135,28 @@ def tile_tnlattention_pb_t_kernel(tc, attn, gate_low, Wg2, Wo, ln_w, ln_b, out):
         ln_w_quad = consts.tile([P, QUAD_TILES, EO], F32)
         ln_b_quad = consts.tile([P, QUAD_TILES, EO], F32)
 
-        def spread_ln_w_and_b():
-            whole = [P, QUAD_TILES, EO]
-            nc.vector.tensor_copy(out=ln_w_quad[:], in_=ln_w_bf16[:].unsqueeze(1).to_broadcast(whole))
-            nc.vector.tensor_copy(out=ln_b_quad[:], in_=ln_b_bf16[:].unsqueeze(1).to_broadcast(whole))
+        wo_grouped = consts.tile([P, EO, PACK], BF16, align_bytes=64)
+        nc.gpsimd.tensor_copy(out=wo_grouped[:], in_=wo_rows[:].rearrange("q t o -> q o t"))
+        whole = [P, QUAD_TILES, EO]
+        nc.gpsimd.tensor_copy(out=ln_w_quad[:], in_=ln_w_bf16[:].unsqueeze(1).to_broadcast(whole))
+        nc.gpsimd.tensor_copy(out=ln_b_quad[:], in_=ln_b_bf16[:].unsqueeze(1).to_broadcast(whole))
 
         def quantise_wo():
-            wo_grouped = consts.tile([P, EO, PACK], BF16, align_bytes=64)
-            nc.vector.tensor_copy(out=wo_grouped[:], in_=wo_rows[:].rearrange("q t o -> q o t"))
             nc.vector.quantize_mx(
                 out=wo_codes[:].bitcast(FP8X4),
                 scales=wo_scales[:],
                 in_=wo_grouped[:].rearrange("q o t -> q (o t)"),
             )
+
+        group_of_pair = {}
+        group_ending = {}
+        for g, (first_pair, n_pairs) in enumerate(GROUPS):
+            for s in range(first_pair, first_pair + n_pairs):
+                group_of_pair[s] = g
+            group_ending[first_pair + n_pairs - 1] = g
+
+        def n_tiles(g):
+            return GROUPS[g][1] * PAIR_TILES
 
         gate_low_t = {}
         gate = {}
@@ -138,15 +169,17 @@ def tile_tnlattention_pb_t_kernel(tc, attn, gate_low, Wg2, Wo, ln_w, ln_b, out):
         rstd = {}
         centred = {}
 
-        def transpose_gate_low(c):
+        def transpose_gate_low(c, tiles):
+            if tiles.start == 0:
+                gate_low_t_sb = gate_low_t_pool.tile([P, CHUNK], BF16)
+                gate_low_t[c] = gate_low_t_sb
             gate_low_t_ps = for_scalar_psum.tile([P, CHUNK], BF16, tag="for_scalar")
-            for j in range(CHUNK_TILES):
+            for j in range(tiles.start, tiles.stop):
                 nc.tensor.transpose(
                     gate_low_t_ps[:, j * P : (j + 1) * P], gate_low_chunks[c][:, j, :], ident_bf16[:]
                 )
-            gate_low_t_sb = gate_low_t_pool.tile([P, CHUNK], BF16)
-            nc.scalar.copy(out=gate_low_t_sb[:], in_=gate_low_t_ps[:])
-            gate_low_t[c] = gate_low_t_sb
+            columns = slice(tiles.start * P, tiles.stop * P)
+            nc.scalar.copy(out=gate_low_t[c][:, columns], in_=gate_low_t_ps[:, columns])
 
         def compute_gate(s):
             c = s // PAIRS_PER_CHUNK
@@ -179,141 +212,153 @@ def tile_tnlattention_pb_t_kernel(tc, attn, gate_low, Wg2, Wo, ln_w, ln_b, out):
             attn_t[s] = attn_t_ps
 
         def multiply(s):
-            quad = s // PAIRS_PER_QUAD
-            if s % PAIRS_PER_QUAD == 0:
+            g = group_of_pair[s]
+            if s == GROUPS[g][0]:
                 h_sb = h_pool.tile([P, QUAD, PACK], BF16, align_bytes=64)
-                h[quad] = h_sb
-            tokens = slice((s % PAIRS_PER_QUAD) * PAIR, (s % PAIRS_PER_QUAD + 1) * PAIR)
-            nc.vector.tensor_tensor(
-                out=h[quad][:, tokens, :].rearrange("q n (u e) -> q n u e", e=2),
-                in0=attn_t[s][:].bitcast(BF16).rearrange("q u (n e) -> q n u e", e=2),
-                in1=gate[s][:].rearrange("q n (u e) -> q n u e", e=2),
-                op=ALU.mult,
-            )
+                h[g] = h_sb
+            first_token = (s - GROUPS[g][0]) * PAIR
+            piece = P if s == 0 else PAIR
+            for n in range(0, PAIR, piece):
+                nc.vector.tensor_tensor(
+                    out=h[g][:, first_token + n : first_token + n + piece, :].rearrange(
+                        "q n (u e) -> q n u e", e=2
+                    ),
+                    in0=attn_t[s][:, :, n : n + piece].bitcast(BF16).rearrange("q u (n e) -> q n u e", e=2),
+                    in1=gate[s][:, n : n + piece, :].rearrange("q n (u e) -> q n u e", e=2),
+                    op=ALU.mult,
+                )
 
-        def quantise(quad):
+        def quantise(g):
             codes = mx_pool.tile([P, QUAD], U32, align_bytes=64)
             scales = mx_pool.tile([P, QUAD], U8, align_bytes=64)
+            tokens = slice(0, n_tiles(g) * P)
             nc.vector.quantize_mx(
-                out=codes[:].bitcast(FP8X4),
-                scales=scales[:],
-                in_=h[quad][:].rearrange("q n t -> q (n t)"),
+                out=codes[:, tokens].bitcast(FP8X4),
+                scales=scales[:, tokens],
+                in_=h[g][:, tokens, :].rearrange("q n t -> q (n t)"),
             )
-            h_codes[quad] = codes
-            h_scales[quad] = scales
+            h_codes[g] = codes
+            h_scales[g] = scales
 
-        def project(quad):
+        def project(g):
             y_ps = y_psum.tile([P, QUAD_TILES, EO], F32)
-            for i in range(QUAD_TILES):
+            for i in range(n_tiles(g)):
                 tokens = slice(i * P, (i + 1) * P)
                 nc.tensor.matmul_mx(
                     out=y_ps[:, i, :],
-                    lhsT=h_codes[quad][:, tokens].bitcast(FP8X4),
-                    lhsT_scale=h_scales[quad][:, tokens],
+                    lhsT=h_codes[g][:, tokens].bitcast(FP8X4),
+                    lhsT_scale=h_scales[g][:, tokens],
                     rhs=wo_codes[:].bitcast(FP8X4),
                     rhs_scale=wo_scales[:],
                     start=True,
                     stop=True,
                 )
-            y[quad] = y_ps
+            y[g] = y_ps
 
-        def statistics(quad):
+        def statistics(g):
             stats_sb = stat_pool.tile([P, QUAD_TILES, BN_VALUES], F32)
-            for i in range(0, QUAD_TILES, 2):
+            for i in range(0, n_tiles(g), 2):
                 nc.vector.bn_stats(
                     out=stats_sb[:, i : i + 2, :].rearrange("p x v -> p (x v)"),
-                    in_=y[quad][:, i : i + 2, :].rearrange("p x o -> p o x"),
+                    in_=y[g][:, i : i + 2, :].rearrange("p x o -> p o x"),
                 )
-            stats[quad] = stats_sb
+            stats[g] = stats_sb
 
-        def compute_rstd(quad):
+        def compute_rstd(g):
+            tiles = slice(0, n_tiles(g))
             var_eps = stat_pool.tile([P, QUAD_TILES], F32)
             nc.scalar.activation(
-                out=var_eps[:], in_=stats[quad][:, :, BN_SUM_OF_SQUARES], func=ACT.Identity,
+                out=var_eps[:, tiles], in_=stats[g][:, tiles, BN_SUM_OF_SQUARES], func=ACT.Identity,
                 bias=LN_EPS, scale=1.0 / EO,
             )
             rstd_sb = stat_pool.tile([P, QUAD_TILES], F32)
-            nc.gpsimd.tensor_tensor(out=rstd_sb[:], in0=var_eps[:], in1=minus_half[:], op=ALU.pow)
-            rstd[quad] = rstd_sb
+            nc.gpsimd.tensor_tensor(
+                out=rstd_sb[:, tiles], in0=var_eps[:, tiles], in1=minus_half[:, tiles], op=ALU.pow
+            )
+            rstd[g] = rstd_sb
 
-        def store(quad, result):
-            first_tile = (quad % QUADS_PER_CHUNK) * QUAD_TILES
+        def store(g, result):
+            chunk, pair_in_chunk = divmod(GROUPS[g][0], PAIRS_PER_CHUNK)
+            first_tile = pair_in_chunk * PAIR_TILES
             nc.sync.dma_start(
-                out=chunk_view(out_rows, quad // QUADS_PER_CHUNK)[:, first_tile : first_tile + QUAD_TILES, :],
-                in_=result[:],
+                out=chunk_view(out_rows, chunk)[:, first_tile : first_tile + n_tiles(g), :],
+                in_=result[:, 0 : n_tiles(g), :],
             )
 
-        def centre(quad):
+        def centre(g):
             centred_sb = result_pool.tile([P, QUAD_TILES, EO], F32)
-            for i in range(QUAD_TILES):
+            for i in range(n_tiles(g)):
                 nc.vector.scalar_tensor_tensor(
-                    out=centred_sb[:, i, :], in0=y[quad][:, i, :],
-                    scalar=stats[quad][:, i, BN_MEAN : BN_MEAN + 1],
+                    out=centred_sb[:, i, :], in0=y[g][:, i, :],
+                    scalar=stats[g][:, i, BN_MEAN : BN_MEAN + 1],
                     in1=ln_w_quad[:, i, :], op0=ALU.subtract, op1=ALU.mult,
                 )
-            centred[quad] = centred_sb
+            centred[g] = centred_sb
 
-        def finish(quad):
+        def finish(g):
             result = result_pool.tile([P, QUAD_TILES, EO], F32)
-            for i in range(QUAD_TILES):
+            for i in range(n_tiles(g)):
                 nc.scalar.activation(
-                    out=result[:, i, :], in_=centred[quad][:, i, :], func=ACT.Copy,
-                    scale=rstd[quad][:, i : i + 1],
+                    out=result[:, i, :], in_=centred[g][:, i, :], func=ACT.Copy,
+                    scale=rstd[g][:, i : i + 1],
                 )
-            nc.gpsimd.tensor_tensor(out=result[:], in0=result[:], in1=ln_b_quad[:], op=ALU.add)
-            store(quad, result)
+            tiles = slice(0, n_tiles(g))
+            nc.gpsimd.tensor_tensor(
+                out=result[:, tiles, :], in0=result[:, tiles, :], in1=ln_b_quad[:, tiles, :], op=ALU.add
+            )
+            store(g, result)
 
-        def finish_on_vector(quad):
+        def finish_on_vector(g):
             result = result_pool.tile([P, QUAD_TILES, EO], F32)
-            for i in range(QUAD_TILES):
+            for i in range(n_tiles(g)):
                 nc.vector.scalar_tensor_tensor(
-                    out=result[:, i, :], in0=centred[quad][:, i, :], scalar=rstd[quad][:, i : i + 1],
+                    out=result[:, i, :], in0=centred[g][:, i, :], scalar=rstd[g][:, i : i + 1],
                     in1=ln_b_quad[:, i, :], op0=ALU.mult, op1=ALU.add,
                 )
-            store(quad, result)
+            store(g, result)
 
         def pair_due(step, lag):
             s = step - lag
             return s if 0 <= s < N_PAIRS else None
 
-        def quad_due(step, lag):
-            quad, rest = divmod(step - lag, PAIRS_PER_QUAD)
-            return quad if rest == 0 and 0 <= quad < N_QUADS else None
+        def group_due(step, lag):
+            return group_ending.get(step - lag)
 
         with tc.manual_schedule():
-            transpose_gate_low(0)
+            transpose_gate_low(0, FIRST_TILES)
             for step in range(N_PAIRS + FINISH_LAG):
                 s = pair_due(step, 0)
                 if s is not None:
                     compute_gate(s)
                     transpose_attn(s)
+                if step == 0:
+                    transpose_gate_low(0, slice(PAIR_TILES, CHUNK_TILES))
                 ahead = pair_due(step, -GATE_LOW_LEAD)
                 if ahead is not None and ahead % PAIRS_PER_CHUNK == 0:
-                    transpose_gate_low(ahead // PAIRS_PER_CHUNK)
-                quad = quad_due(step, PROJECT_LAG)
-                if quad is not None:
-                    project(quad)
-                quad = quad_due(step, RSTD_LAG)
-                if quad is not None:
-                    compute_rstd(quad)
+                    transpose_gate_low(ahead // PAIRS_PER_CHUNK, slice(0, CHUNK_TILES))
+                g = group_due(step, PROJECT_LAG)
+                if g is not None:
+                    project(g)
+                g = group_due(step, RSTD_LAG)
+                if g is not None:
+                    compute_rstd(g)
                 s = pair_due(step, MULTIPLY_LAG)
                 if s is not None:
                     multiply(s)
-                if step == QUANTISE_LAG:
-                    quantise_wo()
-                    spread_ln_w_and_b()
-                quad = quad_due(step, QUANTISE_LAG)
-                if quad is not None:
-                    quantise(quad)
-                quad = quad_due(step, STATS_LAG)
-                if quad is not None:
-                    statistics(quad)
-                quad = quad_due(step, CENTRE_LAG)
-                if quad is not None:
-                    centre(quad)
-                quad = quad_due(step, FINISH_LAG)
-                if quad is not None:
-                    if quad == N_QUADS - 1:
-                        finish_on_vector(quad)
+                g = group_due(step, QUANTISE_LAG)
+                if g is not None:
+                    if g == 0:
+                        quantise_wo()
+                    quantise(g)
+                g = group_due(step, STATS_LAG)
+                if g is not None:
+                    statistics(g)
+                g = group_due(step, CENTRE_LAG)
+                if g is not None:
+                    centre(g)
+                g = group_due(step, FINISH_LAG)
+                if g is not None:
+                    if g >= FIRST_GROUP_BY_VECTOR:
+                        finish_on_vector(g)
                     else:
-                        finish(quad)
+                        finish(g)

@@ -39,16 +39,19 @@ FIRST_TILES = slice(0, PAIR_TILES)
 GATE_LOW_LEAD = 2
 MULTIPLY_LAG = 1
 QUANTISE_LAG = 2
-PROJECT_LAG = 3
-STATS_LAG = 4
-RSTD_LAG = 5
-CENTRE_LAG = 5
-FINISH_LAG = 7
+PROJECT_LAGS = (3, 4)
+STATS_LAG = 5
+RSTD_LAG = 6
+CENTRE_LAG = 6
+FINISH_LAG = 8
 
 GROUPS = [(s, PAIRS_PER_QUAD) for s in range(0, N_PAIRS - PAIRS_PER_QUAD, PAIRS_PER_QUAD)] + [
     (s, 1) for s in range(N_PAIRS - PAIRS_PER_QUAD, N_PAIRS)
 ]
 FIRST_GROUP_BY_VECTOR = len(GROUPS) - 3
+
+WARM_UP_MATMULS = 4
+WARM_UP_WIDTH = 512
 
 FLOPS = 2 * TOKENS * G * E + 2 * TOKENS * E * EO
 
@@ -121,6 +124,11 @@ def tile_tnlattention_pb_t_kernel(tc, attn, gate_low, Wg2, Wo, ln_w, ln_b, out):
         make_identity(nc, ident_f32[:])
         minus_half = consts.tile([P, QUAD_TILES], F32)
         nc.vector.memset(minus_half[:], -0.5)
+        zeros = consts.tile([P, WARM_UP_WIDTH], BF16)
+        nc.vector.memset(zeros[:], 0.0)
+        warm_up_ps = for_scalar_psum.tile([P, WARM_UP_WIDTH], F32, tag="for_scalar")
+        for i in range(WARM_UP_MATMULS):
+            nc.tensor.matmul(out=warm_up_ps[:], lhsT=zeros[:, 0:P], rhs=zeros[:], start=True, stop=True)
         warm = consts.tile([P, 1], F32)
         nc.vector.memset(warm[:], 0.0)
         nc.scalar.activation(out=warm[:], in_=warm[:], func=ACT.Sigmoid)
@@ -240,12 +248,14 @@ def tile_tnlattention_pb_t_kernel(tc, attn, gate_low, Wg2, Wo, ln_w, ln_b, out):
             h_codes[g] = codes
             h_scales[g] = scales
 
-        def project(g):
-            y_ps = y_psum.tile([P, QUAD_TILES, EO], F32)
-            for i in range(n_tiles(g)):
+        def project(g, half):
+            if half == 0:
+                y_ps = y_psum.tile([P, QUAD_TILES, EO], F32)
+                y[g] = y_ps
+            for i in range(half * PAIR_TILES, min((half + 1) * PAIR_TILES, n_tiles(g))):
                 tokens = slice(i * P, (i + 1) * P)
                 nc.tensor.matmul_mx(
-                    out=y_ps[:, i, :],
+                    out=y[g][:, i, :],
                     lhsT=h_codes[g][:, tokens].bitcast(FP8X4),
                     lhsT_scale=h_scales[g][:, tokens],
                     rhs=wo_codes[:].bitcast(FP8X4),
@@ -253,7 +263,6 @@ def tile_tnlattention_pb_t_kernel(tc, attn, gate_low, Wg2, Wo, ln_w, ln_b, out):
                     start=True,
                     stop=True,
                 )
-            y[g] = y_ps
 
         def statistics(g):
             stats_sb = stat_pool.tile([P, QUAD_TILES, BN_VALUES], F32)
@@ -336,9 +345,10 @@ def tile_tnlattention_pb_t_kernel(tc, attn, gate_low, Wg2, Wo, ln_w, ln_b, out):
                 ahead = pair_due(step, -GATE_LOW_LEAD)
                 if ahead is not None and ahead % PAIRS_PER_CHUNK == 0:
                     transpose_gate_low(ahead // PAIRS_PER_CHUNK, slice(0, CHUNK_TILES))
-                g = group_due(step, PROJECT_LAG)
-                if g is not None:
-                    project(g)
+                for half, lag in enumerate(PROJECT_LAGS):
+                    g = group_due(step, lag)
+                    if g is not None:
+                        project(g, half)
                 g = group_due(step, RSTD_LAG)
                 if g is not None:
                     compute_rstd(g)

@@ -36,6 +36,7 @@ BN_MEAN = 1
 BN_SUM_OF_SQUARES = 2
 
 FIRST_TILES = slice(0, PAIR_TILES)
+SECOND_TILES = slice(PAIR_TILES, QUAD_TILES)
 GATE_LOW_LEAD = 2
 MULTIPLY_LAG = 1
 QUANTISE_LAG = 2
@@ -48,10 +49,9 @@ FINISH_LAG = 8
 GROUPS = [(s, PAIRS_PER_QUAD) for s in range(0, N_PAIRS - PAIRS_PER_QUAD, PAIRS_PER_QUAD)] + [
     (s, 1) for s in range(N_PAIRS - PAIRS_PER_QUAD, N_PAIRS)
 ]
-FIRST_GROUP_BY_VECTOR = len(GROUPS) - 3
+FIRST_GROUP_BY_VECTOR = len(GROUPS) - 4
 
-WARM_UP_MATMULS = 4
-WARM_UP_WIDTH = 512
+WARM_UP_MATMULS = 12
 
 FLOPS = 2 * TOKENS * G * E + 2 * TOKENS * E * EO
 
@@ -104,11 +104,11 @@ def tile_tnlattention_pb_t_kernel(tc, attn, gate_low, Wg2, Wo, ln_w, ln_b, out):
                 ],
             )
 
-        load_gate_low(0, FIRST_TILES)
+        load_gate_low(0, slice(0, QUAD_TILES))
         nc.sync.dma_start(out=wg2_sb[:], in_=Wg2[:, :])
         load_attn(0, FIRST_TILES)
-        load_gate_low(0, slice(PAIR_TILES, CHUNK_TILES))
-        load_attn(0, slice(PAIR_TILES, QUAD_TILES))
+        load_gate_low(0, slice(QUAD_TILES, CHUNK_TILES))
+        load_attn(0, SECOND_TILES)
         nc.sync.dma_start(out=wo_rows[:], in_=Wo.rearrange("(q t) o -> q t o", t=PACK))
         load_attn(1, slice(0, QUAD_TILES))
         nc.sync.dma_start(out=ln_w_bf16[:], in_=ln_w.partition_broadcast(P))
@@ -118,17 +118,17 @@ def tile_tnlattention_pb_t_kernel(tc, attn, gate_low, Wg2, Wo, ln_w, ln_b, out):
             for half in range(QUADS_PER_CHUNK):
                 load_attn(c * QUADS_PER_CHUNK + half, slice(0, QUAD_TILES))
 
+        zeros = consts.tile([P, P], BF16)
+        nc.gpsimd.memset(zeros[:], 0.0)
+        warm_up_ps = for_scalar_psum.tile([P, P], F32, tag="for_scalar")
+        for i in range(WARM_UP_MATMULS):
+            nc.tensor.matmul(out=warm_up_ps[:], lhsT=zeros[:], rhs=zeros[:], start=True, stop=True)
         ident_bf16 = consts.tile([P, P], BF16)
         make_identity(nc, ident_bf16[:])
         ident_f32 = consts.tile([P, P], F32)
         make_identity(nc, ident_f32[:])
         minus_half = consts.tile([P, QUAD_TILES], F32)
         nc.vector.memset(minus_half[:], -0.5)
-        zeros = consts.tile([P, WARM_UP_WIDTH], BF16)
-        nc.vector.memset(zeros[:], 0.0)
-        warm_up_ps = for_scalar_psum.tile([P, WARM_UP_WIDTH], F32, tag="for_scalar")
-        for i in range(WARM_UP_MATMULS):
-            nc.tensor.matmul(out=warm_up_ps[:], lhsT=zeros[:, 0:P], rhs=zeros[:], start=True, stop=True)
         warm = consts.tile([P, 1], F32)
         nc.vector.memset(warm[:], 0.0)
         nc.scalar.activation(out=warm[:], in_=warm[:], func=ACT.Sigmoid)
@@ -177,7 +177,7 @@ def tile_tnlattention_pb_t_kernel(tc, attn, gate_low, Wg2, Wo, ln_w, ln_b, out):
         rstd = {}
         centred = {}
 
-        def transpose_gate_low(c, tiles):
+        def transpose_gate_low(c, tiles, copy):
             if tiles.start == 0:
                 gate_low_t_sb = gate_low_t_pool.tile([P, CHUNK], BF16)
                 gate_low_t[c] = gate_low_t_sb
@@ -187,7 +187,7 @@ def tile_tnlattention_pb_t_kernel(tc, attn, gate_low, Wg2, Wo, ln_w, ln_b, out):
                     gate_low_t_ps[:, j * P : (j + 1) * P], gate_low_chunks[c][:, j, :], ident_bf16[:]
                 )
             columns = slice(tiles.start * P, tiles.stop * P)
-            nc.scalar.copy(out=gate_low_t[c][:, columns], in_=gate_low_t_ps[:, columns])
+            copy(out=gate_low_t[c][:, columns], in_=gate_low_t_ps[:, columns])
 
         def compute_gate(s):
             c = s // PAIRS_PER_CHUNK
@@ -225,7 +225,7 @@ def tile_tnlattention_pb_t_kernel(tc, attn, gate_low, Wg2, Wo, ln_w, ln_b, out):
                 h_sb = h_pool.tile([P, QUAD, PACK], BF16, align_bytes=64)
                 h[g] = h_sb
             first_token = (s - GROUPS[g][0]) * PAIR
-            piece = P if s == 0 else PAIR
+            piece = P if s < PAIRS_PER_QUAD else PAIR
             for n in range(0, PAIR, piece):
                 nc.vector.tensor_tensor(
                     out=h[g][:, first_token + n : first_token + n + piece, :].rearrange(
@@ -334,21 +334,25 @@ def tile_tnlattention_pb_t_kernel(tc, attn, gate_low, Wg2, Wo, ln_w, ln_b, out):
             return group_ending.get(step - lag)
 
         with tc.manual_schedule():
-            transpose_gate_low(0, FIRST_TILES)
+            transpose_gate_low(0, FIRST_TILES, nc.scalar.copy)
+            transpose_gate_low(0, SECOND_TILES, nc.vector.tensor_copy)
             for step in range(N_PAIRS + FINISH_LAG):
                 s = pair_due(step, 0)
                 if s is not None:
                     compute_gate(s)
+                    if s == 0:
+                        transpose_gate_low(0, slice(QUAD_TILES, CHUNK_TILES), nc.vector.tensor_copy)
                     transpose_attn(s)
-                if step == 0:
-                    transpose_gate_low(0, slice(PAIR_TILES, CHUNK_TILES))
                 ahead = pair_due(step, -GATE_LOW_LEAD)
                 if ahead is not None and ahead % PAIRS_PER_CHUNK == 0:
-                    transpose_gate_low(ahead // PAIRS_PER_CHUNK, slice(0, CHUNK_TILES))
+                    transpose_gate_low(ahead // PAIRS_PER_CHUNK, slice(0, CHUNK_TILES), nc.scalar.copy)
                 for half, lag in enumerate(PROJECT_LAGS):
                     g = group_due(step, lag)
                     if g is not None:
                         project(g, half)
+                g = group_due(step, FINISH_LAG)
+                if g is not None and g < FIRST_GROUP_BY_VECTOR:
+                    finish(g)
                 g = group_due(step, RSTD_LAG)
                 if g is not None:
                     compute_rstd(g)
@@ -367,8 +371,5 @@ def tile_tnlattention_pb_t_kernel(tc, attn, gate_low, Wg2, Wo, ln_w, ln_b, out):
                 if g is not None:
                     centre(g)
                 g = group_due(step, FINISH_LAG)
-                if g is not None:
-                    if g >= FIRST_GROUP_BY_VECTOR:
-                        finish_on_vector(g)
-                    else:
-                        finish(g)
+                if g is not None and g >= FIRST_GROUP_BY_VECTOR:
+                    finish_on_vector(g)

@@ -44,7 +44,7 @@ PROJECT_LAGS = (3, 4)
 STATS_LAG = 5
 RSTD_LAG = 6
 CENTRE_LAG = 6
-FINISH_LAG = 8
+FINISH_LAG = 10
 
 GROUPS = [(s, PAIRS_PER_QUAD) for s in range(0, N_PAIRS - PAIRS_PER_QUAD, PAIRS_PER_QUAD)] + [
     (s, 1) for s in range(N_PAIRS - PAIRS_PER_QUAD, N_PAIRS)
@@ -252,7 +252,19 @@ def tile_tnlattention_pb_t_kernel(tc, attn, gate_low, Wg2, Wo, ln_w, ln_b, out):
             if half == 0:
                 y_ps = y_psum.tile([P, QUAD_TILES, EO], F32)
                 y[g] = y_ps
-            for i in range(half * PAIR_TILES, min((half + 1) * PAIR_TILES, n_tiles(g))):
+            if half * PAIR_TILES >= n_tiles(g):
+                return
+            two_tiles = slice(half * PAIR, (half + 1) * PAIR)
+            nc.tensor.matmul_mx(
+                out=y[g][:, half * PAIR_TILES : (half + 1) * PAIR_TILES, :].rearrange("p i o -> p (i o)"),
+                lhsT=wo_codes[:].bitcast(FP8X4),
+                lhsT_scale=wo_scales[:],
+                rhs=h_codes[g][:, two_tiles].bitcast(FP8X4),
+                rhs_scale=h_scales[g][:, two_tiles],
+                start=True,
+                stop=True,
+            )
+            for i in range(half * PAIR_TILES, (half + 1) * PAIR_TILES):
                 tokens = slice(i * P, (i + 1) * P)
                 nc.tensor.matmul_mx(
                     out=y[g][:, i, :],

@@ -38,6 +38,7 @@ BN_SUM_OF_SQUARES = 2
 FIRST_TILES = slice(0, PAIR_TILES)
 SECOND_TILES = slice(PAIR_TILES, QUAD_TILES)
 GATE_LOW_LEAD = 2
+SPREAD_STEP = 3
 MULTIPLY_LAG = 1
 QUANTISE_LAG = 2
 PROJECT_LAGS = (3, 4)
@@ -81,8 +82,8 @@ def tile_tnlattention_pb_t_kernel(tc, attn, gate_low, Wg2, Wo, ln_w, ln_b, out):
 
         wg2_sb = consts.tile([P, E], BF16)
         wo_rows = consts.tile([P, PACK, EO], BF16)
-        ln_w_bf16 = consts.tile([P, EO], BF16)
-        ln_b_bf16 = consts.tile([P, EO], BF16)
+        ln_rows = consts.tile([P, 2 * EO], BF16)
+        nc.vector.memset(ln_rows[:], 0.0)
         attn_quads = []
         gate_low_chunks = []
         for c in range(N_CHUNKS):
@@ -111,8 +112,8 @@ def tile_tnlattention_pb_t_kernel(tc, attn, gate_low, Wg2, Wo, ln_w, ln_b, out):
         load_attn(0, SECOND_TILES)
         nc.sync.dma_start(out=wo_rows[:], in_=Wo.rearrange("(q t) o -> q t o", t=PACK))
         load_attn(1, slice(0, QUAD_TILES))
-        nc.sync.dma_start(out=ln_w_bf16[:], in_=ln_w.partition_broadcast(P))
-        nc.sync.dma_start(out=ln_b_bf16[:], in_=ln_b.partition_broadcast(P))
+        nc.sync.dma_start(out=ln_rows[0:1, 0:EO], in_=ln_w.rearrange("(a o) -> a o", a=1))
+        nc.sync.dma_start(out=ln_rows[0:1, EO : 2 * EO], in_=ln_b.rearrange("(a o) -> a o", a=1))
         for c in range(1, N_CHUNKS):
             load_gate_low(c, slice(0, CHUNK_TILES))
             for half in range(QUADS_PER_CHUNK):
@@ -140,14 +141,22 @@ def tile_tnlattention_pb_t_kernel(tc, attn, gate_low, Wg2, Wo, ln_w, ln_b, out):
 
         wo_codes = consts.tile([P, EO], U32, align_bytes=64)
         wo_scales = consts.tile([P, EO], U8, align_bytes=64)
-        ln_w_quad = consts.tile([P, QUAD_TILES, EO], F32)
+        ln_w_and_b = consts.tile([P, 2 * EO], F32)
         ln_b_quad = consts.tile([P, QUAD_TILES, EO], F32)
+        ones = consts.tile([P, P], BF16)
+        nc.vector.memset(ones[:], 1.0)
+
+        def spread_ln_w_and_b():
+            ln_ps = for_scalar_psum.tile([P, 2 * EO], F32, tag="for_scalar")
+            nc.tensor.matmul(out=ln_ps[:], lhsT=ones[:], rhs=ln_rows[:], start=True, stop=True)
+            nc.scalar.copy(out=ln_w_and_b[:], in_=ln_ps[:])
+            nc.gpsimd.tensor_copy(
+                out=ln_b_quad[:],
+                in_=ln_w_and_b[:, EO : 2 * EO].unsqueeze(1).to_broadcast([P, QUAD_TILES, EO]),
+            )
 
         wo_grouped = consts.tile([P, EO, PACK], BF16, align_bytes=64)
         nc.gpsimd.tensor_copy(out=wo_grouped[:], in_=wo_rows[:].rearrange("q t o -> q o t"))
-        whole = [P, QUAD_TILES, EO]
-        nc.gpsimd.tensor_copy(out=ln_w_quad[:], in_=ln_w_bf16[:].unsqueeze(1).to_broadcast(whole))
-        nc.gpsimd.tensor_copy(out=ln_b_quad[:], in_=ln_b_bf16[:].unsqueeze(1).to_broadcast(whole))
 
         def quantise_wo():
             nc.vector.quantize_mx(
@@ -312,7 +321,7 @@ def tile_tnlattention_pb_t_kernel(tc, attn, gate_low, Wg2, Wo, ln_w, ln_b, out):
                 nc.vector.scalar_tensor_tensor(
                     out=centred_sb[:, i, :], in0=y[g][:, i, :],
                     scalar=stats[g][:, i, BN_MEAN : BN_MEAN + 1],
-                    in1=ln_w_quad[:, i, :], op0=ALU.subtract, op1=ALU.mult,
+                    in1=ln_w_and_b[:, 0:EO], op0=ALU.subtract, op1=ALU.mult,
                 )
             centred[g] = centred_sb
 
@@ -355,6 +364,8 @@ def tile_tnlattention_pb_t_kernel(tc, attn, gate_low, Wg2, Wo, ln_w, ln_b, out):
                     if s == 0:
                         transpose_gate_low(0, slice(QUAD_TILES, CHUNK_TILES), nc.vector.tensor_copy)
                     transpose_attn(s)
+                if step == SPREAD_STEP:
+                    spread_ln_w_and_b()
                 ahead = pair_due(step, -GATE_LOW_LEAD)
                 if ahead is not None and ahead % PAIRS_PER_CHUNK == 0:
                     transpose_gate_low(ahead // PAIRS_PER_CHUNK, slice(0, CHUNK_TILES), nc.scalar.copy)

@@ -45,12 +45,13 @@ PROJECT_LAGS = (3, 4)
 STATS_LAG = 5
 RSTD_LAG = 6
 CENTRE_LAG = 6
+NORMALISE_LAG = 8
 FINISH_LAG = 10
 
 GROUPS = [(s, PAIRS_PER_QUAD) for s in range(0, N_PAIRS - PAIRS_PER_QUAD, PAIRS_PER_QUAD)] + [
     (s, 1) for s in range(N_PAIRS - PAIRS_PER_QUAD, N_PAIRS)
 ]
-FIRST_GROUP_BY_VECTOR = len(GROUPS) - 4
+FIRST_GROUP_BY_VECTOR = len(GROUPS) - 5
 
 WARM_UP_MATMULS = 12
 
@@ -74,8 +75,8 @@ def tile_tnlattention_pb_t_kernel(tc, attn, gate_low, Wg2, Wo, ln_w, ln_b, out):
         gate_pool = ctx.enter_context(tc.tile_pool(name="gate", bufs=3))
         h_pool = ctx.enter_context(tc.tile_pool(name="h", bufs=3))
         mx_pool = ctx.enter_context(tc.tile_pool(name="mx", bufs=3))
-        stat_pool = ctx.enter_context(tc.tile_pool(name="stat", bufs=4))
-        result_pool = ctx.enter_context(tc.tile_pool(name="result", bufs=6))
+        stat_pool = ctx.enter_context(tc.tile_pool(name="stat", bufs=6))
+        result_pool = ctx.enter_context(tc.tile_pool(name="result", bufs=8))
         for_scalar_psum = ctx.enter_context(tc.psum_pool(name="for_scalar_ps", bufs=3))
         attn_t_psum = ctx.enter_context(tc.psum_pool(name="attn_t_ps", bufs=2))
         y_psum = ctx.enter_context(tc.psum_pool(name="y_ps", bufs=3))
@@ -142,6 +143,7 @@ def tile_tnlattention_pb_t_kernel(tc, attn, gate_low, Wg2, Wo, ln_w, ln_b, out):
         wo_codes = consts.tile([P, EO], U32, align_bytes=64)
         wo_scales = consts.tile([P, EO], U8, align_bytes=64)
         ln_w_and_b = consts.tile([P, 2 * EO], F32)
+        ln_w_quad = consts.tile([P, QUAD_TILES, EO], F32)
         ln_b_quad = consts.tile([P, QUAD_TILES, EO], F32)
         ones = consts.tile([P, P], BF16)
         nc.vector.memset(ones[:], 1.0)
@@ -150,6 +152,9 @@ def tile_tnlattention_pb_t_kernel(tc, attn, gate_low, Wg2, Wo, ln_w, ln_b, out):
             ln_ps = for_scalar_psum.tile([P, 2 * EO], F32, tag="for_scalar")
             nc.tensor.matmul(out=ln_ps[:], lhsT=ones[:], rhs=ln_rows[:], start=True, stop=True)
             nc.scalar.copy(out=ln_w_and_b[:], in_=ln_ps[:])
+            nc.gpsimd.tensor_copy(
+                out=ln_w_quad[:], in_=ln_w_and_b[:, 0:EO].unsqueeze(1).to_broadcast([P, QUAD_TILES, EO])
+            )
             nc.gpsimd.tensor_copy(
                 out=ln_b_quad[:],
                 in_=ln_w_and_b[:, EO : 2 * EO].unsqueeze(1).to_broadcast([P, QUAD_TILES, EO]),
@@ -184,7 +189,12 @@ def tile_tnlattention_pb_t_kernel(tc, attn, gate_low, Wg2, Wo, ln_w, ln_b, out):
         y = {}
         stats = {}
         rstd = {}
+        shift = {}
         centred = {}
+        normalised = {}
+
+        def is_light_on_vector(g):
+            return g % 3 == 1 and g < FIRST_GROUP_BY_VECTOR - 1
 
         def transpose_gate_low(c, tiles, copy):
             if tiles.start == 0:
@@ -198,6 +208,10 @@ def tile_tnlattention_pb_t_kernel(tc, attn, gate_low, Wg2, Wo, ln_w, ln_b, out):
             columns = slice(tiles.start * P, tiles.stop * P)
             copy(out=gate_low_t[c][:, columns], in_=gate_low_t_ps[:, columns])
 
+        def pieces(s):
+            halves = [(0, P // 2), (P // 2, P)] if s == 0 else [(0, P)]
+            return halves + [(P, PAIR)]
+
         def compute_gate(s):
             c = s // PAIRS_PER_CHUNK
             first_tile = (s % PAIRS_PER_CHUNK) * PAIR_TILES
@@ -210,11 +224,13 @@ def tile_tnlattention_pb_t_kernel(tc, attn, gate_low, Wg2, Wo, ln_w, ln_b, out):
                         out=z_ps[:, t, :], lhsT=wg2_by_t[:, t, :], rhs=gate_low_t[c][:, tokens],
                         start=True, stop=True,
                     )
-                nc.scalar.activation(
-                    out=gate_sb[:, i * P : (i + 1) * P, :],
-                    in_=z_ps[:].rearrange("q t n -> q n t"),
-                    func=ACT.Sigmoid,
-                )
+                for start, stop in pieces(s):
+                    if start // P == i:
+                        nc.scalar.activation(
+                            out=gate_sb[:, start:stop, :],
+                            in_=z_ps[:, :, start - i * P : stop - i * P].rearrange("q t n -> q n t"),
+                            func=ACT.Sigmoid,
+                        )
             gate[s] = gate_sb
 
         def transpose_attn(s):
@@ -234,14 +250,13 @@ def tile_tnlattention_pb_t_kernel(tc, attn, gate_low, Wg2, Wo, ln_w, ln_b, out):
                 h_sb = h_pool.tile([P, QUAD, PACK], BF16, align_bytes=64)
                 h[g] = h_sb
             first_token = (s - GROUPS[g][0]) * PAIR
-            piece = P if s < PAIRS_PER_QUAD else PAIR
-            for n in range(0, PAIR, piece):
+            for start, stop in pieces(s) if s < PAIRS_PER_QUAD else [(0, PAIR)]:
                 nc.vector.tensor_tensor(
-                    out=h[g][:, first_token + n : first_token + n + piece, :].rearrange(
+                    out=h[g][:, first_token + start : first_token + stop, :].rearrange(
                         "q n (u e) -> q n u e", e=2
                     ),
-                    in0=attn_t[s][:, :, n : n + piece].bitcast(BF16).rearrange("q u (n e) -> q n u e", e=2),
-                    in1=gate[s][:, n : n + piece, :].rearrange("q n (u e) -> q n u e", e=2),
+                    in0=attn_t[s][:, :, start:stop].bitcast(BF16).rearrange("q u (n e) -> q n u e", e=2),
+                    in1=gate[s][:, start:stop, :].rearrange("q n (u e) -> q n u e", e=2),
                     op=ALU.mult,
                 )
 
@@ -306,6 +321,12 @@ def tile_tnlattention_pb_t_kernel(tc, attn, gate_low, Wg2, Wo, ln_w, ln_b, out):
                 out=rstd_sb[:, tiles], in0=var_eps[:, tiles], in1=minus_half[:, tiles], op=ALU.pow
             )
             rstd[g] = rstd_sb
+            if is_light_on_vector(g):
+                neg_mean = stat_pool.tile([P, QUAD_TILES], F32)
+                nc.scalar.mul(out=neg_mean[:], in_=stats[g][:, :, BN_MEAN], mul=-1.0)
+                shift_sb = stat_pool.tile([P, QUAD_TILES], F32)
+                nc.gpsimd.tensor_tensor(out=shift_sb[:], in0=neg_mean[:], in1=rstd_sb[:], op=ALU.mult)
+                shift[g] = shift_sb
 
         def store(g, result):
             chunk, pair_in_chunk = divmod(GROUPS[g][0], PAIRS_PER_CHUNK)
@@ -325,13 +346,28 @@ def tile_tnlattention_pb_t_kernel(tc, attn, gate_low, Wg2, Wo, ln_w, ln_b, out):
                 )
             centred[g] = centred_sb
 
-        def finish(g):
-            result = result_pool.tile([P, QUAD_TILES, EO], F32)
-            for i in range(n_tiles(g)):
+        def normalise(g):
+            normalised_sb = result_pool.tile([P, QUAD_TILES, EO], F32)
+            for i in range(QUAD_TILES):
                 nc.scalar.activation(
-                    out=result[:, i, :], in_=centred[g][:, i, :], func=ACT.Copy,
-                    scale=rstd[g][:, i : i + 1],
+                    out=normalised_sb[:, i, :], in_=y[g][:, i, :], func=ACT.Identity,
+                    bias=shift[g][:, i : i + 1], scale=rstd[g][:, i : i + 1],
                 )
+            nc.gpsimd.tensor_tensor(
+                out=normalised_sb[:], in0=normalised_sb[:], in1=ln_w_quad[:], op=ALU.mult
+            )
+            normalised[g] = normalised_sb
+
+        def finish(g):
+            if is_light_on_vector(g):
+                result = normalised[g]
+            else:
+                result = result_pool.tile([P, QUAD_TILES, EO], F32)
+                for i in range(n_tiles(g)):
+                    nc.scalar.activation(
+                        out=result[:, i, :], in_=centred[g][:, i, :], func=ACT.Copy,
+                        scale=rstd[g][:, i : i + 1],
+                    )
             tiles = slice(0, n_tiles(g))
             nc.gpsimd.tensor_tensor(
                 out=result[:, tiles, :], in0=result[:, tiles, :], in1=ln_b_quad[:, tiles, :], op=ALU.add
@@ -355,7 +391,8 @@ def tile_tnlattention_pb_t_kernel(tc, attn, gate_low, Wg2, Wo, ln_w, ln_b, out):
             return group_ending.get(step - lag)
 
         with tc.manual_schedule():
-            transpose_gate_low(0, FIRST_TILES, nc.scalar.copy)
+            transpose_gate_low(0, slice(0, 1), nc.scalar.copy)
+            transpose_gate_low(0, slice(1, PAIR_TILES), nc.vector.tensor_copy)
             transpose_gate_low(0, SECOND_TILES, nc.vector.tensor_copy)
             for step in range(N_PAIRS + FINISH_LAG):
                 s = pair_due(step, 0)
@@ -373,12 +410,21 @@ def tile_tnlattention_pb_t_kernel(tc, attn, gate_low, Wg2, Wo, ln_w, ln_b, out):
                     g = group_due(step, lag)
                     if g is not None:
                         project(g, half)
+                g = group_due(step, RSTD_LAG)
+                if g is not None and step < N_PAIRS:
+                    compute_rstd(g)
+                g = group_due(step, NORMALISE_LAG)
+                if g is not None and is_light_on_vector(g):
+                    normalise(g)
                 g = group_due(step, FINISH_LAG)
                 if g is not None and g < FIRST_GROUP_BY_VECTOR:
                     finish(g)
                 g = group_due(step, RSTD_LAG)
-                if g is not None:
+                if g is not None and step >= N_PAIRS:
                     compute_rstd(g)
+                g = group_due(step, STATS_LAG)
+                if g is not None and g >= FIRST_GROUP_BY_VECTOR:
+                    statistics(g)
                 s = pair_due(step, MULTIPLY_LAG)
                 if s is not None:
                     multiply(s)
@@ -388,10 +434,10 @@ def tile_tnlattention_pb_t_kernel(tc, attn, gate_low, Wg2, Wo, ln_w, ln_b, out):
                         quantise_wo()
                     quantise(g)
                 g = group_due(step, STATS_LAG)
-                if g is not None:
+                if g is not None and g < FIRST_GROUP_BY_VECTOR:
                     statistics(g)
                 g = group_due(step, CENTRE_LAG)
-                if g is not None:
+                if g is not None and not is_light_on_vector(g):
                     centre(g)
                 g = group_due(step, FINISH_LAG)
                 if g is not None and g >= FIRST_GROUP_BY_VECTOR:

from contextlib import ExitStack

import concourse.mybir as mybir
from concourse.masks import make_identity

F32 = mybir.dt.float32
BF16 = mybir.dt.bfloat16
U32 = mybir.dt.uint32
U8 = mybir.dt.uint8
FP8X4 = mybir.dt.float8_e4m3fn_x4
ACT = mybir.ActivationFunctionType
ALU = mybir.AluOpType

P = 128
PACK = 4
TOKENS = 4 * 2048
E = 512
G = 128
EO = 128
LN_EPS = 1e-5

PAIR_TILES = 2
QUAD_TILES = 4
CHUNK_TILES = 8
PAIR = PAIR_TILES * P
QUAD = QUAD_TILES * P
CHUNK = CHUNK_TILES * P
N_CHUNKS = TOKENS // CHUNK
N_QUADS = TOKENS // QUAD
N_PAIRS = TOKENS // PAIR
PAIRS_PER_CHUNK = CHUNK_TILES // PAIR_TILES
PAIRS_PER_QUAD = QUAD_TILES // PAIR_TILES
QUADS_PER_CHUNK = CHUNK_TILES // QUAD_TILES
BN_VALUES = 3
BN_MEAN = 1
BN_SUM_OF_SQUARES = 2

FIRST_TILES = slice(0, PAIR_TILES)
SECOND_TILES = slice(PAIR_TILES, QUAD_TILES)
GATE_LOW_LEAD = 2
SPREAD_STEP = 3
MULTIPLY_LAG = 1
QUANTISE_LAG = 2
PROJECT_LAGS = (3, 4)
STATS_LAG = 5
RSTD_LAG = 6
CENTRE_LAG = 6
NORMALISE_LAG = 8
FINISH_LAG = 10

GROUPS = [(s, PAIRS_PER_QUAD) for s in range(0, N_PAIRS - PAIRS_PER_QUAD, PAIRS_PER_QUAD)] + [
    (s, 1) for s in range(N_PAIRS - PAIRS_PER_QUAD, N_PAIRS)
]
FIRST_GROUP_BY_VECTOR = len(GROUPS) - 5

WARM_UP_MATMULS = 12

FLOPS = 2 * TOKENS * G * E + 2 * TOKENS * E * EO


def tile_tnlattention_pb_t_kernel(tc, attn, gate_low, Wg2, Wo, ln_w, ln_b, out):
    nc = tc.nc
    attn_rows = attn.flatten_outer_dims()
    gate_low_rows = gate_low.flatten_outer_dims()
    out_rows = out.flatten_outer_dims()

    def chunk_view(rows, c):
        return rows[c * CHUNK : (c + 1) * CHUNK, :].rearrange("(p j) w -> p j w", j=CHUNK_TILES)

    with ExitStack() as ctx:
        consts = ctx.enter_context(tc.tile_pool(name="consts", bufs=1))
        attn_pool = ctx.enter_context(tc.tile_pool(name="attn", bufs=N_QUADS))
        gate_low_pool = ctx.enter_context(tc.tile_pool(name="gate_low", bufs=N_CHUNKS))
        gate_low_t_pool = ctx.enter_context(tc.tile_pool(name="gate_low_t", bufs=2))
        gate_pool = ctx.enter_context(tc.tile_pool(name="gate", bufs=3))
        h_pool = ctx.enter_context(tc.tile_pool(name="h", bufs=3))
        mx_pool = ctx.enter_context(tc.tile_pool(name="mx", bufs=3))
        stat_pool = ctx.enter_context(tc.tile_pool(name="stat", bufs=6))
        result_pool = ctx.enter_context(tc.tile_pool(name="result", bufs=8))
        for_scalar_psum = ctx.enter_context(tc.psum_pool(name="for_scalar_ps", bufs=3))
        attn_t_psum = ctx.enter_context(tc.psum_pool(name="attn_t_ps", bufs=2))
        y_psum = ctx.enter_context(tc.psum_pool(name="y_ps", bufs=3))

        wg2_sb = consts.tile([P, E], BF16)
        wo_rows = consts.tile([P, PACK, EO], BF16)
        ln_rows = consts.tile([P, 2 * EO], BF16)
        nc.vector.memset(ln_rows[:], 0.0)
        attn_quads = []
        gate_low_chunks = []
        for c in range(N_CHUNKS):
            gate_low_sb = gate_low_pool.tile([P, CHUNK_TILES, G], BF16)
            gate_low_chunks.append(gate_low_sb)
            for half in range(QUADS_PER_CHUNK):
                attn_sb = attn_pool.tile([P, QUAD_TILES, E], BF16)
                attn_quads.append(attn_sb)

        def load_gate_low(c, tiles):
            nc.sync.dma_start(out=gate_low_chunks[c][:, tiles, :], in_=chunk_view(gate_low_rows, c)[:, tiles, :])

        def load_attn(quad, tiles):
            first_tile = (quad % QUADS_PER_CHUNK) * QUAD_TILES
            nc.sync.dma_start(
                out=attn_quads[quad][:, tiles, :],
                in_=chunk_view(attn_rows, quad // QUADS_PER_CHUNK)[
                    :, first_tile + tiles.start : first_tile + tiles.stop, :
                ],
            )

        load_gate_low(0, slice(0, QUAD_TILES))
        nc.sync.dma_start(out=wg2_sb[:], in_=Wg2[:, :])
        load_attn(0, FIRST_TILES)
        load_gate_low(0, slice(QUAD_TILES, CHUNK_TILES))
        load_attn(0, SECOND_TILES)
        nc.sync.dma_start(out=wo_rows[:], in_=Wo.rearrange("(q t) o -> q t o", t=PACK))
        load_attn(1, slice(0, QUAD_TILES))
        nc.sync.dma_start(out=ln_rows[0:1, 0:EO], in_=ln_w.rearrange("(a o) -> a o", a=1))
        nc.sync.dma_start(out=ln_rows[0:1, EO : 2 * EO], in_=ln_b.rearrange("(a o) -> a o", a=1))
        for c in range(1, N_CHUNKS):
            load_gate_low(c, slice(0, CHUNK_TILES))
            for half in range(QUADS_PER_CHUNK):
                load_attn(c * QUADS_PER_CHUNK + half, slice(0, QUAD_TILES))

        zeros = consts.tile([P, P], BF16)
        nc.gpsimd.memset(zeros[:], 0.0)
        warm_up_ps = for_scalar_psum.tile([P, P], F32, tag="for_scalar")
        for i in range(WARM_UP_MATMULS):
            nc.tensor.matmul(out=warm_up_ps[:], lhsT=zeros[:], rhs=zeros[:], start=True, stop=True)
        ident_bf16 = consts.tile([P, P], BF16)
        make_identity(nc, ident_bf16[:])
        ident_f32 = consts.tile([P, P], F32)
        make_identity(nc, ident_f32[:])
        minus_half = consts.tile([P, QUAD_TILES], F32)
        nc.vector.memset(minus_half[:], -0.5)
        warm = consts.tile([P, 1], F32)
        nc.vector.memset(warm[:], 0.0)
        nc.scalar.activation(out=warm[:], in_=warm[:], func=ACT.Sigmoid)

        wg2_by_t = consts.tile([P, PACK, P], BF16)
        nc.vector.tensor_copy(
            out=wg2_by_t[:], in_=wg2_sb[:].rearrange("g (q t) -> g t q", t=PACK)
        )

        wo_codes = consts.tile([P, EO], U32, align_bytes=64)
        wo_scales = consts.tile([P, EO], U8, align_bytes=64)
        ln_w_and_b = consts.tile([P, 2 * EO], F32)
        ln_w_quad = consts.tile([P, QUAD_TILES, EO], F32)
        ln_b_quad = consts.tile([P, QUAD_TILES, EO], F32)
        ones = consts.tile([P, P], BF16)
        nc.vector.memset(ones[:], 1.0)

        def spread_ln_w_and_b():
            ln_ps = for_scalar_psum.tile([P, 2 * EO], F32, tag="for_scalar")
            nc.tensor.matmul(out=ln_ps[:], lhsT=ones[:], rhs=ln_rows[:], start=True, stop=True)
            nc.scalar.copy(out=ln_w_and_b[:], in_=ln_ps[:])
            nc.gpsimd.tensor_copy(
                out=ln_w_quad[:], in_=ln_w_and_b[:, 0:EO].unsqueeze(1).to_broadcast([P, QUAD_TILES, EO])
            )
            nc.gpsimd.tensor_copy(
                out=ln_b_quad[:],
                in_=ln_w_and_b[:, EO : 2 * EO].unsqueeze(1).to_broadcast([P, QUAD_TILES, EO]),
            )

        wo_grouped = consts.tile([P, EO, PACK], BF16, align_bytes=64)
        nc.gpsimd.tensor_copy(out=wo_grouped[:], in_=wo_rows[:].rearrange("q t o -> q o t"))

        def quantise_wo():
            nc.vector.quantize_mx(
                out=wo_codes[:].bitcast(FP8X4),
                scales=wo_scales[:],
                in_=wo_grouped[:].rearrange("q o t -> q (o t)"),
            )

        group_of_pair = {}
        group_ending = {}
        for g, (first_pair, n_pairs) in enumerate(GROUPS):
            for s in range(first_pair, first_pair + n_pairs):
                group_of_pair[s] = g
            group_ending[first_pair + n_pairs - 1] = g

        def n_tiles(g):
            return GROUPS[g][1] * PAIR_TILES

        gate_low_t = {}
        gate = {}
        attn_t = {}
        h = {}
        h_codes = {}
        h_scales = {}
        y = {}
        stats = {}
        rstd = {}
        shift = {}
        centred = {}
        normalised = {}

        def is_light_on_vector(g):
            return g % 3 == 1 and g < FIRST_GROUP_BY_VECTOR - 1

        def transpose_gate_low(c, tiles, copy):
            if tiles.start == 0:
                gate_low_t_sb = gate_low_t_pool.tile([P, CHUNK], BF16)
                gate_low_t[c] = gate_low_t_sb
            gate_low_t_ps = for_scalar_psum.tile([P, CHUNK], BF16, tag="for_scalar")
            for j in range(tiles.start, tiles.stop):
                nc.tensor.transpose(
                    gate_low_t_ps[:, j * P : (j + 1) * P], gate_low_chunks[c][:, j, :], ident_bf16[:]
                )
            columns = slice(tiles.start * P, tiles.stop * P)
            copy(out=gate_low_t[c][:, columns], in_=gate_low_t_ps[:, columns])

        def pieces(s):
            halves = [(0, P // 2), (P // 2, P)] if s == 0 else [(0, P)]
            return halves + [(P, PAIR)]

        def compute_gate(s):
            c = s // PAIRS_PER_CHUNK
            first_tile = (s % PAIRS_PER_CHUNK) * PAIR_TILES
            gate_sb = gate_pool.tile([P, PAIR, PACK], F32)
            for i in range(PAIR_TILES):
                tokens = slice((first_tile + i) * P, (first_tile + i + 1) * P)
                z_ps = for_scalar_psum.tile([P, PACK, P], F32, tag="for_scalar")
                for t in range(PACK):
                    nc.tensor.matmul(
                        out=z_ps[:, t, :], lhsT=wg2_by_t[:, t, :], rhs=gate_low_t[c][:, tokens],
                        start=True, stop=True,
                    )
                for start, stop in pieces(s):
                    if start // P == i:
                        nc.scalar.activation(
                            out=gate_sb[:, start:stop, :],
                            in_=z_ps[:, :, start - i * P : stop - i * P].rearrange("q t n -> q n t"),
                            func=ACT.Sigmoid,
                        )
            gate[s] = gate_sb

        def transpose_attn(s):
            first_tile = (s % PAIRS_PER_QUAD) * PAIR_TILES
            attn_t_ps = attn_t_psum.tile([P, 2, PAIR], F32)
            for i in range(PAIR_TILES):
                words = attn_quads[s // PAIRS_PER_QUAD][:, first_tile + i, :].bitcast(F32)
                for u in range(2):
                    nc.tensor.transpose(
                        attn_t_ps[:, u, i * P : (i + 1) * P], words[:, u : 2 * P : 2], ident_f32[:]
                    )
            attn_t[s] = attn_t_ps

        def multiply(s):
            g = group_of_pair[s]
            if s == GROUPS[g][0]:
                h_sb = h_pool.tile([P, QUAD, PACK], BF16, align_bytes=64)
                h[g] = h_sb
            first_token = (s - GROUPS[g][0]) * PAIR
            for start, stop in pieces(s) if s < PAIRS_PER_QUAD else [(0, PAIR)]:
                nc.vector.tensor_tensor(
                    out=h[g][:, first_token + start : first_token + stop, :].rearrange(
                        "q n (u e) -> q n u e", e=2
                    ),
                    in0=attn_t[s][:, :, start:stop].bitcast(BF16).rearrange("q u (n e) -> q n u e", e=2),
                    in1=gate[s][:, start:stop, :].rearrange("q n (u e) -> q n u e", e=2),
                    op=ALU.mult,
                )

        def quantise(g):
            codes = mx_pool.tile([P, QUAD], U32, align_bytes=64)
            scales = mx_pool.tile([P, QUAD], U8, align_bytes=64)
            tokens = slice(0, n_tiles(g) * P)
            nc.vector.quantize_mx(
                out=codes[:, tokens].bitcast(FP8X4),
                scales=scales[:, tokens],
                in_=h[g][:, tokens, :].rearrange("q n t -> q (n t)"),
            )
            h_codes[g] = codes
            h_scales[g] = scales

        def project(g, half):
            if half == 0:
                y_ps = y_psum.tile([P, QUAD_TILES, EO], F32)
                y[g] = y_ps
            if half * PAIR_TILES >= n_tiles(g):
                return
            two_tiles = slice(half * PAIR, (half + 1) * PAIR)
            nc.tensor.matmul_mx(
                out=y[g][:, half * PAIR_TILES : (half + 1) * PAIR_TILES, :].rearrange("p i o -> p (i o)"),
                lhsT=wo_codes[:].bitcast(FP8X4),
                lhsT_scale=wo_scales[:],
                rhs=h_codes[g][:, two_tiles].bitcast(FP8X4),
                rhs_scale=h_scales[g][:, two_tiles],
                start=True,
                stop=True,
            )
            for i in range(half * PAIR_TILES, (half + 1) * PAIR_TILES):
                tokens = slice(i * P, (i + 1) * P)
                nc.tensor.matmul_mx(
                    out=y[g][:, i, :],
                    lhsT=h_codes[g][:, tokens].bitcast(FP8X4),
                    lhsT_scale=h_scales[g][:, tokens],
                    rhs=wo_codes[:].bitcast(FP8X4),
                    rhs_scale=wo_scales[:],
                    start=True,
                    stop=True,
                )

        def statistics(g):
            stats_sb = stat_pool.tile([P, QUAD_TILES, BN_VALUES], F32)
            for i in range(0, n_tiles(g), 2):
                nc.vector.bn_stats(
                    out=stats_sb[:, i : i + 2, :].rearrange("p x v -> p (x v)"),
                    in_=y[g][:, i : i + 2, :].rearrange("p x o -> p o x"),
                )
            stats[g] = stats_sb

        def compute_rstd(g):
            tiles = slice(0, n_tiles(g))
            var_eps = stat_pool.tile([P, QUAD_TILES], F32)
            nc.scalar.activation(
                out=var_eps[:, tiles], in_=stats[g][:, tiles, BN_SUM_OF_SQUARES], func=ACT.Identity,
                bias=LN_EPS, scale=1.0 / EO,
            )
            rstd_sb = stat_pool.tile([P, QUAD_TILES], F32)
            nc.gpsimd.tensor_tensor(
                out=rstd_sb[:, tiles], in0=var_eps[:, tiles], in1=minus_half[:, tiles], op=ALU.pow
            )
            rstd[g] = rstd_sb
            if is_light_on_vector(g):
                neg_mean = stat_pool.tile([P, QUAD_TILES], F32)
                nc.scalar.mul(out=neg_mean[:], in_=stats[g][:, :, BN_MEAN], mul=-1.0)
                shift_sb = stat_pool.tile([P, QUAD_TILES], F32)
                nc.gpsimd.tensor_tensor(out=shift_sb[:], in0=neg_mean[:], in1=rstd_sb[:], op=ALU.mult)
                shift[g] = shift_sb

        def store(g, result):
            chunk, pair_in_chunk = divmod(GROUPS[g][0], PAIRS_PER_CHUNK)
            first_tile = pair_in_chunk * PAIR_TILES
            nc.sync.dma_start(
                out=chunk_view(out_rows, chunk)[:, first_tile : first_tile + n_tiles(g), :],
                in_=result[:, 0 : n_tiles(g), :],
            )

        def centre(g):
            centred_sb = result_pool.tile([P, QUAD_TILES, EO], F32)
            for i in range(n_tiles(g)):
                nc.vector.scalar_tensor_tensor(
                    out=centred_sb[:, i, :], in0=y[g][:, i, :],
                    scalar=stats[g][:, i, BN_MEAN : BN_MEAN + 1],
                    in1=ln_w_and_b[:, 0:EO], op0=ALU.subtract, op1=ALU.mult,
                )
            centred[g] = centred_sb

        def normalise(g):
            normalised_sb = result_pool.tile([P, QUAD_TILES, EO], F32)
            for i in range(QUAD_TILES):
                nc.scalar.activation(
                    out=normalised_sb[:, i, :], in_=y[g][:, i, :], func=ACT.Identity,
                    bias=shift[g][:, i : i + 1], scale=rstd[g][:, i : i + 1],
                )
            nc.gpsimd.tensor_tensor(
                out=normalised_sb[:], in0=normalised_sb[:], in1=ln_w_quad[:], op=ALU.mult
            )
            normalised[g] = normalised_sb

        def finish(g):
            if is_light_on_vector(g):
                result = normalised[g]
            else:
                result = result_pool.tile([P, QUAD_TILES, EO], F32)
                for i in range(n_tiles(g)):
                    nc.scalar.activation(
                        out=result[:, i, :], in_=centred[g][:, i, :], func=ACT.Copy,
                        scale=rstd[g][:, i : i + 1],
                    )
            tiles = slice(0, n_tiles(g))
            nc.gpsimd.tensor_tensor(
                out=result[:, tiles, :], in0=result[:, tiles, :], in1=ln_b_quad[:, tiles, :], op=ALU.add
            )
            store(g, result)

        def finish_on_vector(g):
            result = result_pool.tile([P, QUAD_TILES, EO], F32)
            for i in range(n_tiles(g)):
                nc.vector.scalar_tensor_tensor(
                    out=result[:, i, :], in0=centred[g][:, i, :], scalar=rstd[g][:, i : i + 1],
                    in1=ln_b_quad[:, i, :], op0=ALU.mult, op1=ALU.add,
                )
            store(g, result)

        def pair_due(step, lag):
            s = step - lag
            return s if 0 <= s < N_PAIRS else None

        def group_due(step, lag):
            return group_ending.get(step - lag)

        with tc.manual_schedule():
            transpose_gate_low(0, slice(0, 1), nc.scalar.copy)
            transpose_gate_low(0, slice(1, PAIR_TILES), nc.vector.tensor_copy)
            transpose_gate_low(0, SECOND_TILES, nc.vector.tensor_copy)
            for step in range(N_PAIRS + FINISH_LAG):
                s = pair_due(step, 0)
                if s is not None:
                    compute_gate(s)
                    if s == 0:
                        transpose_gate_low(0, slice(QUAD_TILES, CHUNK_TILES), nc.vector.tensor_copy)
                    transpose_attn(s)
                if step == SPREAD_STEP:
                    spread_ln_w_and_b()
                ahead = pair_due(step, -GATE_LOW_LEAD)
                if ahead is not None and ahead % PAIRS_PER_CHUNK == 0:
                    transpose_gate_low(ahead // PAIRS_PER_CHUNK, slice(0, CHUNK_TILES), nc.scalar.copy)
                for half, lag in enumerate(PROJECT_LAGS):
                    g = group_due(step, lag)
                    if g is not None:
                        project(g, half)
                g = group_due(step, RSTD_LAG)
                if g is not None and step < N_PAIRS:
                    compute_rstd(g)
                g = group_due(step, NORMALISE_LAG)
                if g is not None and is_light_on_vector(g):
                    normalise(g)
                g = group_due(step, FINISH_LAG)
                if g is not None and g < FIRST_GROUP_BY_VECTOR:
                    finish(g)
                g = group_due(step, RSTD_LAG)
                if g is not None and step >= N_PAIRS:
                    compute_rstd(g)
                g = group_due(step, STATS_LAG)
                if g is not None and g >= FIRST_GROUP_BY_VECTOR:
                    statistics(g)
                s = pair_due(step, MULTIPLY_LAG)
                if s is not None:
                    multiply(s)
                g = group_due(step, QUANTISE_LAG)
                if g is not None:
                    if g == 0:
                        quantise_wo()
                    quantise(g)
                g = group_due(step, STATS_LAG)
                if g is not None and g < FIRST_GROUP_BY_VECTOR:
                    statistics(g)
                g = group_due(step, CENTRE_LAG)
                if g is not None and not is_light_on_vector(g):
                    centre(g)
                g = group_due(step, FINISH_LAG)
                if g is not None and g >= FIRST_GROUP_BY_VECTOR:
                    finish_on_vector(g)
